import numpy as np
import ml_dtypes


def mxq(x, axis, fmt="e4m3"):
    dtype, down = {"e4m3": (ml_dtypes.float8_e4m3fn, 7), "e5m2": (ml_dtypes.float8_e5m2, 14)}[fmt]
    v = np.moveaxis(np.asarray(x, np.float32).astype(ml_dtypes.bfloat16).astype(np.float64), axis, -1)
    blocks = v.reshape(v.shape[:-1] + (-1, 32))
    amax = np.abs(blocks).max(-1, keepdims=True)
    byte = np.maximum(np.where(amax > 0, np.frexp(amax)[1] - 1 + 127, 0) - down, 1)
    scale = np.exp2(byte - 127.0)
    codes = (blocks / scale).astype(np.float32).astype(dtype).astype(np.float64)
    return np.moveaxis((codes * scale).reshape(v.shape), -1, axis)


WIDE = False


def mx_kscale(k):
    if not WIDE:
        return np.ones(k)
    levels = np.array([10, -10, 5, -5, 0])
    if k % 512:
        return np.exp2(np.random.permutation(np.resize(levels, k // 32))).repeat(32)
    a = np.empty((k // 512, 16))
    for p in range(k // 512):
        a[p, :8] = np.random.permutation(np.resize(levels, 8))
        for g in range(8):
            far = levels[np.abs(levels - a[p, g]) >= 10]
            a[p, g + 8] = far[np.random.randint(len(far))]
    return np.exp2(a.ravel()).repeat(32)


BF16 = ml_dtypes.bfloat16


def bf(x):
    return np.asarray(x, np.float32).astype(BF16)


def f64(x):
    return np.asarray(x).astype(np.float64)


B, L, LV, H = 32, 32, 64, 1024
NUM_ITERATIONS = 3
X = 0.25
V = 0.12 * L
A = 0.6 / (np.sqrt(H) * V)


def draw0():
    s = mx_kscale(H)
    return {"text_feat": bf(np.random.standard_normal((B, L, H)) * X * s),
            "vision_proj": bf(np.random.standard_normal((B, 1, H)) * V),
            "Wt": bf(np.random.standard_normal((H, H)) * A / (X * np.sqrt(H)) / s[None, :]),
            "bt": bf(np.random.standard_normal(H) * 0.5 * A)}


def core(text_feat, vision_proj, Wt, bt):
    vp = f64(vision_proj)
    text_proj = (mxq(f64(text_feat), 2, "e4m3") @ mxq(f64(Wt), 1, "e4m3").T) + f64(bt)
    agreement = np.sum(text_proj * vp, axis=-1, keepdims=True)
    coupling = np.zeros_like(agreement)
    for _ in range(NUM_ITERATIONS - 1):
        coupling = coupling + agreement
    e = np.exp(coupling - coupling.max(axis=1, keepdims=True))
    routing_weights = e / e.sum(axis=1, keepdims=True)
    weighted_vision = routing_weights * vp
    return text_proj, weighted_vision


def e4m3fn_bytes(y):
    return np.clip(np.asarray(y, np.float64), -448.0, 448.0).astype(np.float32).astype(ml_dtypes.float8_e4m3fn).view(np.uint8)


def e4m3fn_values(b):
    return np.asarray(b, np.uint8).view(ml_dtypes.float8_e4m3fn).astype(np.float64)


def setup_inputs():
    d = draw0()
    x0 = np.asarray(d['text_feat']).astype(np.float64)
    s = (np.max(np.abs(x0), axis=(0, 1), keepdims=True) / 448.0).astype(np.float32)
    out = {}
    for k, v in d.items():
        if k == 'text_feat':
            out['text_feat_bytes'] = e4m3fn_bytes(x0 / s.astype(np.float64))
            out['text_feat_scale'] = s
        else:
            out[k] = v
    return out


def reference(text_feat_bytes, text_feat_scale, vision_proj, Wt, bt):
    return core(e4m3fn_values(text_feat_bytes) * text_feat_scale.astype(np.float64), vision_proj, Wt, bt)

@@ -1,0 +1,405 @@
+from contextlib import ExitStack
+
+import concourse.mybir as mybir
+from concourse.masks import make_block_diagonal, make_identity
+
+FLOPS = 2 * 1024 * 1024 * 1024
+
+F32 = mybir.dt.float32
+BF16 = mybir.dt.bfloat16
+U32 = mybir.dt.uint32
+U8 = mybir.dt.uint8
+FP8 = mybir.dt.float8_e4m3fn
+FP8X4 = mybir.dt.float8_e4m3fn_x4
+ALU = mybir.AluOpType
+ACT = mybir.ActivationFunctionType
+AX = mybir.AxisListType
+
+P = 128
+H = 1024
+BANK = 512
+GROUPS = 4
+LAST = GROUPS - 1
+SPAN = 16
+BATCHES = P // SPAN
+W_TILES = H // P
+PER_PARTITION = H // P
+PASS_WORDS = 256
+TILE_CODES = 2 * P
+BANK_ORDER = ((0, 1), (1, 1), (0, 0), (1, 0))
+W_TILES_BEFORE = (3, 1, 2, 2)
+
+
+def tile_dynamicroutingfusion_pa_kernel(
+    tc, text_feat_bytes, text_feat_scale, vision_proj, Wt, bt, out_0, out_1
+):
+    nc = tc.nc
+    with ExitStack() as ctx:
+        keep = ctx.enter_context(tc.tile_pool(name="keep", bufs=1))
+        outs = ctx.enter_context(tc.tile_pool(name="outs", bufs=6))
+        prods = ctx.enter_context(tc.tile_pool(name="prods", bufs=4))
+        small = ctx.enter_context(tc.tile_pool(name="small", bufs=2))
+        psum = ctx.enter_context(tc.psum_pool(name="psum", bufs=8))
+
+        bytes_view = text_feat_bytes.flatten_outer_dims().rearrange("(g p c) k -> g p (c k)", p=P, c=2)
+        text_proj_view = out_0.flatten_outer_dims().rearrange("(g p c) h -> g c p h", p=P, c=2)
+        weighted_view = out_1.flatten_outer_dims().rearrange("(g p c) h -> g c p h", p=P, c=2)
+
+        scale_all = keep.tile([P, H], F32, name="scale_all")
+        bias_all = keep.tile([P, H], BF16, name="bias_all")
+        vision = keep.tile([P, GROUPS, H], BF16, name="vision")
+        x_bytes, x_scaled, x_grouped, x_codes, x_scales = [], [], [], [], []
+        for g in range(GROUPS):
+            x_bytes_g = keep.tile([P, 2 * H], U8, name="x_bytes%d" % g)
+            x_scaled_g = keep.tile([P, 2 * H], BF16, name="x_scaled%d" % g)
+            x_grouped_g = keep.tile([P, 2 * H], BF16, name="x_grouped%d" % g, align_bytes=64)
+            x_codes_g = keep.tile([P, 2 * TILE_CODES], U32, name="x_codes%d" % g, align_bytes=64)
+            x_scales_g = keep.tile([P, 2 * TILE_CODES], U8, name="x_scales%d" % g, align_bytes=64)
+            x_bytes.append(x_bytes_g)
+            x_scaled.append(x_scaled_g)
+            x_grouped.append(x_grouped_g)
+            x_codes.append(x_codes_g)
+            x_scales.append(x_scales_g)
+        w_rows = []
+        for j in range(W_TILES):
+            w_rows_j = keep.tile([P, H], BF16, name="w_rows%d" % j)
+            w_rows.append(w_rows_j)
+        w_grouped, w_codes, w_scales = [], [], []
+        for hf in range(2):
+            w_grouped_h = keep.tile([P, 4 * H], BF16, name="w_grouped%d" % hf, align_bytes=64)
+            w_codes_h = keep.tile([P, H], U32, name="w_codes%d" % hf, align_bytes=64)
+            w_scales_h = keep.tile([P, H], U8, name="w_scales%d" % hf, align_bytes=64)
+            w_grouped.append(w_grouped_h)
+            w_codes.append(w_codes_h)
+            w_scales.append(w_scales_h)
+
+        scale_cols = keep.tile([P, PER_PARTITION], F32, name="scale_cols")
+        nc.sync.dma_start(out=scale_cols[:], in_=text_feat_scale.rearrange("a b (p q) -> (a b p) q", q=PER_PARTITION))
+        bias_cols = keep.tile([P, PER_PARTITION], BF16, name="bias_cols")
+        nc.sync.dma_start(out=bias_cols[:], in_=bt.rearrange("(p q) -> p q", q=PER_PARTITION))
+        nc.sync.dma_start(out=x_bytes[0][:], in_=bytes_view[0])
+        for j in range(W_TILES):
+            nc.sync.dma_start(out=w_rows[j][:], in_=Wt[P * j : P * (j + 1), :])
+            if j == W_TILES_BEFORE[0] - 1:
+                nc.sync.dma_start(out=x_bytes[1][:], in_=bytes_view[1])
+        vision_rows = keep.tile([P, H], BF16, name="vision_rows")
+        nc.vector.memset(vision_rows[:], 0.0)
+        nc.sync.dma_start(out=vision_rows[0:BATCHES, :], in_=vision_proj[0:BATCHES].rearrange("b o h -> (b o) h"))
+        nc.sync.dma_start(out=x_bytes[2][:], in_=bytes_view[2])
+        nc.sync.dma_start(out=x_bytes[3][:], in_=bytes_view[3])
+        vision_by_batch = vision_proj.rearrange("(g e) o h -> e (o g) h", e=BATCHES)
+        for low in range(4):
+            for high in range(4):
+                r = 4 * high + low
+                nc.sync.dma_start(out=vision[r:P:SPAN, 1:GROUPS, :], in_=vision_by_batch[:, 1:GROUPS, :])
+
+        ident = keep.tile([P, P], F32, name="ident")
+        make_identity(nc, ident[:])
+        zero = keep.tile([P, 1], F32, name="zero")
+        nc.vector.memset(zero[:], 0.0)
+        warm = keep.tile([P, 1], F32, name="warm")
+        nc.scalar.activation(out=warm[:], in_=zero[:], func=ACT.Exp)
+        ident_bf = keep.tile([P, P], BF16, name="ident_bf")
+        make_identity(nc, ident_bf[:])
+        pick = keep.tile([P, P], BF16, name="pick")
+        nc.gpsimd.memset(pick[:], 0.0)
+        nc.gpsimd.affine_select(
+            out=pick[:], in_=pick[:], compare_op=ALU.not_equal, fill=1.0, base=0,
+            pattern=[[-1, BATCHES], [0, SPAN]], channel_multiplier=1,
+        )
+        same_batch = keep.tile([P, P], F32, name="same_batch")
+        make_block_diagonal(nc, same_batch[:], SPAN)
+        place = keep.tile([P, SPAN], F32, name="place")
+        nc.vector.tensor_reduce(out=place[:], in_=ident[:].rearrange("p (e n) -> p n e", n=SPAN), axis=AX.X, op=ALU.add)
+
+        def spread_scales():
+            dst = scale_all[:].rearrange("p (r part q) -> p part r q", part=2, q=4)
+            for part in range(2):
+                s_ps = psum.tile([P, BANK], F32, name="s_ps", tag="bank")
+                for q in range(4):
+                    col = scale_cols[:, 4 * part + q : 4 * part + q + 1]
+                    nc.tensor.transpose(s_ps[:, P * q : P * (q + 1)], col.to_broadcast([P, P]), ident[:])
+                in_k_order = s_ps[:].rearrange("p (q r) -> p r q", q=4)
+                if part == 0:
+                    nc.vector.tensor_copy(out=dst[:, part], in_=in_k_order)
+                else:
+                    nc.scalar.copy(out=dst[:, part], in_=in_k_order)
+
+        def spread_bias():
+            b_ps = psum.tile([P, H], BF16, name="b_ps", tag="bank")
+            for q in range(PER_PARTITION):
+                nc.tensor.transpose(b_ps[:, P * q : P * (q + 1)], bias_cols[:, q : q + 1].to_broadcast([P, P]), ident_bf[:])
+            nc.scalar.copy(
+                out=bias_all[:].rearrange("p (r q) -> p r q", q=PER_PARTITION),
+                in_=b_ps[:].rearrange("p (q r) -> p r q", q=PER_PARTITION),
+            )
+
+        def spread_vision_of_group_0():
+            v_ps = psum.tile([P, H], BF16, name="v_ps", tag="bank")
+            for hf in range(2):
+                cols = slice(BANK * hf, BANK * (hf + 1))
+                nc.tensor.matmul(out=v_ps[:, cols], lhsT=pick[:], rhs=vision_rows[:, cols], start=True, stop=True)
+            nc.scalar.copy(out=vision[:, 0, :], in_=v_ps[:])
+
+        def turn(rows_as_words, grouped_as_words):
+            t_ps = psum.tile([P, BANK], F32, name="t_ps", tag="bank")
+            for i in range(2):
+                for u in range(2):
+                    slot = 2 * i + u
+                    nc.tensor.transpose(
+                        t_ps[:, P * slot : P * (slot + 1)],
+                        rows_as_words[:, PASS_WORDS * i + u : PASS_WORDS * (i + 1) : 2],
+                        ident[:],
+                    )
+            nc.scalar.copy(out=grouped_as_words, in_=t_ps[:].rearrange("p (i u r) -> p i r u", i=2, u=2))
+
+        def turn_w(j):
+            hf, place_in_half = divmod(j, W_TILES // 2)
+            dst = w_grouped[hf][:].bitcast(F32).rearrange("p (i h u) -> p i h u", i=2, u=2)
+            turn(w_rows[j][:].bitcast(F32), dst[:, :, P * place_in_half : P * (place_in_half + 1), :])
+
+        def quantize_w(hf):
+            nc.vector.quantize_mx(out=w_codes[hf][:].bitcast(FP8X4), scales=w_scales[hf][:], in_=w_grouped[hf][:])
+
+        def widen_x(g, c):
+            cols = slice(H * c, H * (c + 1))
+            nc.vector.tensor_tensor(
+                out=x_scaled[g][:, cols], in0=x_bytes[g][:, cols].bitcast(FP8), in1=scale_all[:], op=ALU.mult
+            )
+
+        def turn_x(g, c):
+            cols = slice(H * c, H * (c + 1))
+            dst = x_grouped[g][:, cols].bitcast(F32).rearrange("p (i r u) -> p i r u", i=2, u=2)
+            turn(x_scaled[g][:, cols].bitcast(F32), dst)
+
+        def quantize_x(g):
+            nc.vector.quantize_mx(out=x_codes[g][:].bitcast(FP8X4), scales=x_scales[g][:], in_=x_grouped[g][:])
+
+        bank_of = {}
+        text_proj_of = {}
+        products_of = {}
+        softmax_of = {}
+
+        def project_group(g):
+            for c, hf in BANK_ORDER:
+                p_ps = psum.tile([P, BANK], F32, name="p_ps", tag="bank")
+                for i in range(2):
+                    x_cols = slice(TILE_CODES * c + P * i, TILE_CODES * c + P * (i + 1))
+                    w_cols = slice(BANK * i, BANK * (i + 1))
+                    nc.tensor.matmul_mx(
+                        out=p_ps[:],
+                        lhsT=x_codes[g][:, x_cols].bitcast(FP8X4),
+                        lhsT_scale=x_scales[g][:, x_cols],
+                        rhs=w_codes[hf][:, w_cols].bitcast(FP8X4),
+                        rhs_scale=w_scales[hf][:, w_cols],
+                        start=(i == 0),
+                        stop=(i == 1),
+                    )
+                bank_of[(g, c, hf)] = p_ps
+
+        def open_group(g):
+            for c in range(2):
+                text_proj = outs.tile([P, H], F32, name="text_proj")
+                text_proj_of[(g, c)] = text_proj
+            minus_2a = small.tile([P, 2], F32, name="minus_2a")
+            softmax_of[(g, "minus_2a")] = minus_2a
+
+        def open_products(g):
+            for c in range(2):
+                products = prods.tile([P, H], F32, name="products")
+                products_of[(g, c)] = products
+
+        def add_bias(g, c, hf):
+            cols = slice(BANK * hf, BANK * (hf + 1))
+            nc.vector.tensor_tensor(
+                out=text_proj_of[(g, c)][:, cols], in0=bank_of[(g, c, hf)][:], in1=bias_all[:, cols], op=ALU.add
+            )
+
+        def store_text_proj(g, c):
+            nc.sync.dma_start(out=text_proj_view[g, c], in_=text_proj_of[(g, c)][:])
+
+        def multiply_on_vector(g, c):
+            nc.vector.tensor_tensor(
+                out=products_of[(g, c)][:, 0:BANK], in0=bank_of[(g, c, 0)][:], in1=vision[:, g, 0:BANK], op=ALU.mult
+            )
+
+        def multiply_on_gpsimd(g, c):
+            nc.gpsimd.tensor_tensor(
+                out=products_of[(g, c)][:, BANK:H], in0=text_proj_of[(g, c)][:, BANK:H], in1=vision[:, g, BANK:H],
+                op=ALU.mult,
+            )
+
+        def sum_on_scalar(g, c):
+            unused = small.tile([P, H], BF16, name="unused")
+            nc.scalar.activation(
+                out=unused[:], in_=products_of[(g, c)][:], func=ACT.Copy, scale=-2.0,
+                accum_out=softmax_of[(g, "minus_2a")][:, c : c + 1],
+            )
+
+        def multiply_and_sum_on_vector(partial, g, c, hf):
+            cols = slice(BANK * hf, BANK * (hf + 1))
+            unused_half = small.tile([P, BANK], BF16, name="unused_half")
+            nc.vector.scalar_tensor_tensor(
+                out=unused_half[:], in0=bank_of[(g, c, hf)][:], scalar=-2.0, in1=vision[:, g, cols],
+                op0=ALU.mult, op1=ALU.mult, accum_out=partial[:, 2 * c + hf : 2 * c + hf + 1],
+            )
+
+        def gather_batch(g):
+            minus_2a = softmax_of[(g, "minus_2a")]
+            placed = small.tile([P, 2 * SPAN], F32, name="placed")
+            for c in range(2):
+                nc.gpsimd.tensor_scalar(
+                    out=placed[:, SPAN * c : SPAN * (c + 1)], in0=place[:], scalar1=minus_2a[:, c : c + 1], scalar2=0.0,
+                    op0=ALU.mult, op1=ALU.add,
+                )
+            own = psum.tile([P, 2 * SPAN], F32, name="own", tag="bank")
+            nc.tensor.matmul(out=own[:], lhsT=same_batch[:], rhs=placed[:], start=True, stop=True)
+            softmax_of[(g, "own")] = own
+
+        def exponentials(g):
+            minus_m = small.tile([P, 1], F32, name="minus_m")
+            nc.vector.tensor_reduce(out=minus_m[:], in_=softmax_of[(g, "own")][:], axis=AX.X, op=ALU.min)
+            terms = small.tile([P, 2 * SPAN], F32, name="terms")
+            den = small.tile([P, 1], F32, name="den")
+            nc.scalar.activation(
+                out=terms[:], in_=softmax_of[(g, "own")][:], func=ACT.Exp, bias=minus_m[:], scale=-1.0, accum_out=den[:]
+            )
+            num = small.tile([P, 2], F32, name="num")
+            nc.scalar.activation(
+                out=num[:], in_=softmax_of[(g, "minus_2a")][:], func=ACT.Exp, bias=minus_m[:], scale=-1.0
+            )
+            softmax_of[(g, "den")] = den
+            softmax_of[(g, "num")] = num
+
+        def reciprocal_of_den(g):
+            inv_den = small.tile([P, 1], F32, name="inv_den")
+            nc.vector.reciprocal(out=inv_den[:], in_=softmax_of[(g, "den")][:])
+            routing = small.tile([P, 2], F32, name="routing")
+            softmax_of[(g, "routing")] = routing
+            return inv_den
+
+        def routing_on_scalar(g):
+            inv_den = reciprocal_of_den(g)
+            nc.scalar.activation(
+                out=softmax_of[(g, "routing")][:], in_=softmax_of[(g, "num")][:], func=ACT.Copy, scale=inv_den[:, 0:1]
+            )
+
+        def routing_on_vector(g):
+            inv_den = reciprocal_of_den(g)
+            nc.vector.tensor_scalar(
+                out=softmax_of[(g, "routing")][:], in0=softmax_of[(g, "num")][:], scalar1=inv_den[:, 0:1], scalar2=None,
+                op0=ALU.mult,
+            )
+
+        def weigh_on_scalar(weighted, g, c, cols):
+            nc.scalar.activation(
+                out=weighted[:, cols], in_=vision[:, g, cols], func=ACT.Copy,
+                scale=softmax_of[(g, "routing")][:, c : c + 1],
+            )
+            nc.scalar.dma_start(out=weighted_view[g, c][:, cols], in_=weighted[:, cols])
+
+        def weigh_on_gpsimd(weighted, g, c, cols):
+            nc.gpsimd.tensor_scalar(
+                out=weighted[:, cols], in0=vision[:, g, cols], scalar1=softmax_of[(g, "routing")][:, c : c + 1],
+                scalar2=0.0, op0=ALU.mult, op1=ALU.add,
+            )
+
+        def weigh_group(g):
+            weighted_0 = outs.tile([P, H], F32, name="weighted")
+            weigh_on_scalar(weighted_0, g, 0, slice(0, H))
+            weighted_1 = outs.tile([P, H], F32, name="weighted")
+            weigh_on_gpsimd(weighted_1, g, 1, slice(0, H))
+            return weighted_1
+
+        def store_weighted(weighted, g, c, cols):
+            nc.sync.dma_start(out=weighted_view[g, c][:, cols], in_=weighted[:, cols])
+
+        with tc.manual_schedule():
+            spread_scales()
+            j = 0
+            for tile_no in range(len(W_TILES_BEFORE)):
+                for count in range(W_TILES_BEFORE[tile_no]):
+                    turn_w(j)
+                    j += 1
+                widen_x(tile_no // 2, tile_no % 2)
+                turn_x(tile_no // 2, tile_no % 2)
+            quantize_x(0)
+            widen_x(2, 0)
+            turn_x(2, 0)
+            widen_x(2, 1)
+            turn_x(2, 1)
+            spread_bias()
+            spread_vision_of_group_0()
+            widen_x(3, 0)
+            quantize_x(1)
+            turn_x(3, 0)
+            widen_x(3, 1)
+            turn_x(3, 1)
+            quantize_w(0)
+            quantize_w(1)
+            project_group(0)
+            quantize_x(2)
+            quantize_x(3)
+            project_group(1)
+
+            open_group(0)
+            open_products(0)
+            add_bias(0, 0, 1)
+            multiply_on_gpsimd(0, 0)
+            for g in range(LAST):
+                add_bias(g, 1, 1)
+                multiply_on_gpsimd(g, 1)
+                multiply_on_vector(g, 0)
+                sum_on_scalar(g, 0)
+                multiply_on_vector(g, 1)
+                if g > 0:
+                    exponentials(g - 1)
+                sum_on_scalar(g, 1)
+                open_group(g + 1)
+                if g + 1 < LAST:
+                    open_products(g + 1)
+                    add_bias(g + 1, 0, 1)
+                    multiply_on_gpsimd(g + 1, 0)
+                gather_batch(g)
+                add_bias(g, 0, 0)
+                store_text_proj(g, 0)
+                add_bias(g, 1, 0)
+                store_text_proj(g, 1)
+                if g > 0:
+                    routing_on_scalar(g - 1)
+                    weighted_1 = weigh_group(g - 1)
+                    store_weighted(weighted_1, g - 1, 1, slice(0, H))
+                if g + 2 < GROUPS:
+                    project_group(g + 2)
+
+            partial = keep.tile([P, 4], F32, name="partial")
+            for c, hf in BANK_ORDER[0:3]:
+                multiply_and_sum_on_vector(partial, LAST, c, hf)
+            exponentials(LAST - 1)
+            for c, hf in BANK_ORDER[3:4]:
+                multiply_and_sum_on_vector(partial, LAST, c, hf)
+            routing_on_scalar(LAST - 1)
+            nc.gpsimd.tensor_tensor(
+                out=softmax_of[(LAST, "minus_2a")][:], in0=partial[:, 0:4:2], in1=partial[:, 1:4:2], op=ALU.add
+            )
+            gather_batch(LAST)
+            weighted_1 = weigh_group(LAST - 1)
+            add_bias(LAST, 0, 1)
+            add_bias(LAST, 0, 0)
+            store_text_proj(LAST, 0)
+            exponentials(LAST)
+            add_bias(LAST, 1, 1)
+            store_weighted(weighted_1, LAST - 1, 1, slice(0, H))
+            routing_on_vector(LAST)
+            weighted_1 = outs.tile([P, H], F32, name="weighted")
+            nc.vector.tensor_scalar(
+                out=weighted_1[:], in0=vision[:, LAST, :], scalar1=softmax_of[(LAST, "routing")][:, 1:2], scalar2=None,
+                op0=ALU.mult,
+            )
+            store_weighted(weighted_1, LAST, 1, slice(0, H))
+            weighted_0 = outs.tile([P, H], F32, name="weighted")
+            weigh_on_scalar(weighted_0, LAST, 0, slice(0, BANK))
+            weigh_on_gpsimd(weighted_0, LAST, 0, slice(BANK, H))
+            store_weighted(weighted_0, LAST, 0, slice(BANK, H))
+            add_bias(LAST, 1, 0)
+            store_text_proj(LAST, 1)

@@ -218,6 +218,11 @@ def tile_dynamicroutingfusion_pa_kernel(
         def store_text_proj(g, c):
             nc.sync.dma_start(out=text_proj_view[g, c], in_=text_proj_of[(g, c)][:])
 
+        def add_bias_and_store(g, c, hf):
+            add_bias(g, c, hf)
+            cols = slice(BANK * hf, BANK * (hf + 1))
+            nc.sync.dma_start(out=text_proj_view[g, c][:, cols], in_=text_proj_of[(g, c)][:, cols])
+
         def multiply_on_vector(g, c):
             nc.vector.tensor_tensor(
                 out=products_of[(g, c)][:, 0:BANK], in0=bank_of[(g, c, 0)][:], in1=vision[:, g, 0:BANK], op=ALU.mult
@@ -236,6 +241,13 @@ def tile_dynamicroutingfusion_pa_kernel(
                 accum_out=softmax_of[(g, "minus_2a")][:, c : c + 1],
             )
 
+        def sum_upper_on_scalar(partial, g, c):
+            unused = small.tile([P, H], BF16, name="unused")
+            nc.scalar.activation(
+                out=unused[:, BANK:H], in_=products_of[(g, c)][:, BANK:H], func=ACT.Copy, scale=-2.0,
+                accum_out=partial[:, 2 * c + 1 : 2 * c + 2],
+            )
+
         def multiply_and_sum_on_vector(partial, g, c, hf):
             cols = slice(BANK * hf, BANK * (hf + 1))
             unused_half = small.tile([P, BANK], BF16, name="unused_half")
@@ -248,9 +260,8 @@ def tile_dynamicroutingfusion_pa_kernel(
             minus_2a = softmax_of[(g, "minus_2a")]
             placed = small.tile([P, 2 * SPAN], F32, name="placed")
             for c in range(2):
-                nc.gpsimd.tensor_scalar(
-                    out=placed[:, SPAN * c : SPAN * (c + 1)], in0=place[:], scalar1=minus_2a[:, c : c + 1], scalar2=0.0,
-                    op0=ALU.mult, op1=ALU.add,
+                nc.scalar.activation(
+                    out=placed[:, SPAN * c : SPAN * (c + 1)], in_=place[:], func=ACT.Copy, scale=minus_2a[:, c : c + 1]
                 )
             own = psum.tile([P, 2 * SPAN], F32, name="own", tag="bank")
             nc.tensor.matmul(out=own[:], lhsT=same_batch[:], rhs=placed[:], start=True, stop=True)
@@ -304,9 +315,18 @@ def tile_dynamicroutingfusion_pa_kernel(
                 scalar2=0.0, op0=ALU.mult, op1=ALU.add,
             )
 
-        def weigh_group(g):
-            weighted_0 = outs.tile([P, H], F32, name="weighted")
-            weigh_on_scalar(weighted_0, g, 0, slice(0, H))
+        def weigh_on_vector(g, c):
+            weighted = outs.tile([P, H], F32, name="weighted")
+            nc.vector.tensor_scalar(
+                out=weighted[:], in0=vision[:, g, :], scalar1=softmax_of[(g, "routing")][:, c : c + 1], scalar2=None,
+                op0=ALU.mult,
+            )
+            store_weighted(weighted, g, c, slice(0, H))
+
+        def weigh_group(g, both=True):
+            if both:
+                weighted_0 = outs.tile([P, H], F32, name="weighted")
+                weigh_on_scalar(weighted_0, g, 0, slice(0, H))
             weighted_1 = outs.tile([P, H], F32, name="weighted")
             weigh_on_gpsimd(weighted_1, g, 1, slice(0, H))
             return weighted_1
@@ -329,14 +349,14 @@ def tile_dynamicroutingfusion_pa_kernel(
             widen_x(2, 1)
             turn_x(2, 1)
             spread_bias()
-            spread_vision_of_group_0()
             widen_x(3, 0)
             quantize_x(1)
             turn_x(3, 0)
             widen_x(3, 1)
             turn_x(3, 1)
-            quantize_w(0)
+            spread_vision_of_group_0()
             quantize_w(1)
+            quantize_w(0)
             project_group(0)
             quantize_x(2)
             quantize_x(3)
@@ -344,10 +364,10 @@ def tile_dynamicroutingfusion_pa_kernel(
 
             open_group(0)
             open_products(0)
-            add_bias(0, 0, 1)
+            add_bias_and_store(0, 0, 1)
             multiply_on_gpsimd(0, 0)
             for g in range(LAST):
-                add_bias(g, 1, 1)
+                add_bias_and_store(g, 1, 1)
                 multiply_on_gpsimd(g, 1)
                 multiply_on_vector(g, 0)
                 sum_on_scalar(g, 0)
@@ -356,50 +376,44 @@ def tile_dynamicroutingfusion_pa_kernel(
                     exponentials(g - 1)
                 sum_on_scalar(g, 1)
                 open_group(g + 1)
-                if g + 1 < LAST:
-                    open_products(g + 1)
-                    add_bias(g + 1, 0, 1)
-                    multiply_on_gpsimd(g + 1, 0)
+                open_products(g + 1)
+                add_bias_and_store(g + 1, 0, 1)
+                multiply_on_gpsimd(g + 1, 0)
                 gather_batch(g)
-                add_bias(g, 0, 0)
-                store_text_proj(g, 0)
-                add_bias(g, 1, 0)
-                store_text_proj(g, 1)
+                add_bias_and_store(g, 0, 0)
+                add_bias_and_store(g, 1, 0)
+                if g + 1 == LAST:
+                    add_bias_and_store(LAST, 1, 1)
+                    multiply_on_gpsimd(LAST, 1)
                 if g > 0:
                     routing_on_scalar(g - 1)
-                    weighted_1 = weigh_group(g - 1)
-                    store_weighted(weighted_1, g - 1, 1, slice(0, H))
+                    weighted_1 = weigh_group(g - 1, g < LAST - 1)
+                    if g < LAST - 1:
+                        store_weighted(weighted_1, g - 1, 1, slice(0, H))
                 if g + 2 < GROUPS:
                     project_group(g + 2)
 
             partial = keep.tile([P, 4], F32, name="partial")
-            for c, hf in BANK_ORDER[0:3]:
-                multiply_and_sum_on_vector(partial, LAST, c, hf)
+            multiply_and_sum_on_vector(partial, LAST, 0, 0)
+            multiply_and_sum_on_vector(partial, LAST, 1, 0)
+            sum_upper_on_scalar(partial, LAST, 0)
             exponentials(LAST - 1)
-            for c, hf in BANK_ORDER[3:4]:
-                multiply_and_sum_on_vector(partial, LAST, c, hf)
+            sum_upper_on_scalar(partial, LAST, 1)
+            add_bias_and_store(LAST, 0, 0)
             routing_on_scalar(LAST - 1)
-            nc.gpsimd.tensor_tensor(
+            store_weighted(weighted_1, LAST - 2, 1, slice(0, H))
+            weigh_on_vector(LAST - 2, 0)
+            nc.vector.tensor_tensor(
                 out=softmax_of[(LAST, "minus_2a")][:], in0=partial[:, 0:4:2], in1=partial[:, 1:4:2], op=ALU.add
             )
             gather_batch(LAST)
             weighted_1 = weigh_group(LAST - 1)
-            add_bias(LAST, 0, 1)
-            add_bias(LAST, 0, 0)
-            store_text_proj(LAST, 0)
-            exponentials(LAST)
-            add_bias(LAST, 1, 1)
+            add_bias_and_store(LAST, 1, 0)
             store_weighted(weighted_1, LAST - 1, 1, slice(0, H))
+            exponentials(LAST)
             routing_on_vector(LAST)
-            weighted_1 = outs.tile([P, H], F32, name="weighted")
-            nc.vector.tensor_scalar(
-                out=weighted_1[:], in0=vision[:, LAST, :], scalar1=softmax_of[(LAST, "routing")][:, 1:2], scalar2=None,
-                op0=ALU.mult,
-            )
-            store_weighted(weighted_1, LAST, 1, slice(0, H))
+            weigh_on_vector(LAST, 1)
             weighted_0 = outs.tile([P, H], F32, name="weighted")
             weigh_on_scalar(weighted_0, LAST, 0, slice(0, BANK))
             weigh_on_gpsimd(weighted_0, LAST, 0, slice(BANK, H))
             store_weighted(weighted_0, LAST, 0, slice(BANK, H))
-            add_bias(LAST, 1, 0)
-            store_text_proj(LAST, 1)

@@ -39,7 +39,9 @@ def tile_dynamicroutingfusion_pa_kernel(
         outs = ctx.enter_context(tc.tile_pool(name="outs", bufs=6))
         prods = ctx.enter_context(tc.tile_pool(name="prods", bufs=4))
         small = ctx.enter_context(tc.tile_pool(name="small", bufs=2))
-        psum = ctx.enter_context(tc.psum_pool(name="psum", bufs=8))
+        uppers = ctx.enter_context(tc.psum_pool(name="uppers", bufs=4))
+        lowers = ctx.enter_context(tc.psum_pool(name="lowers", bufs=3))
+        owns = ctx.enter_context(tc.psum_pool(name="owns", bufs=1))
 
         bytes_view = text_feat_bytes.flatten_outer_dims().rearrange("(g p c) k -> g p (c k)", p=P, c=2)
         text_proj_view = out_0.flatten_outer_dims().rearrange("(g p c) h -> g c p h", p=P, c=2)
@@ -112,10 +114,16 @@ def tile_dynamicroutingfusion_pa_kernel(
         place = keep.tile([P, SPAN], F32, name="place")
         nc.vector.tensor_reduce(out=place[:], in_=ident[:].rearrange("p (e n) -> p n e", n=SPAN), axis=AX.X, op=ALU.add)
 
+        banks_taken = [0]
+
+        def head_bank():
+            banks_taken[0] += 1
+            return (uppers, lowers)[banks_taken[0] % 2]
+
         def spread_scales():
             dst = scale_all[:].rearrange("p (r part q) -> p part r q", part=2, q=4)
             for part in range(2):
-                s_ps = psum.tile([P, BANK], F32, name="s_ps", tag="bank")
+                s_ps = head_bank().tile([P, BANK], F32, name="s_ps", tag="bank")
                 for q in range(4):
                     col = scale_cols[:, 4 * part + q : 4 * part + q + 1]
                     nc.tensor.transpose(s_ps[:, P * q : P * (q + 1)], col.to_broadcast([P, P]), ident[:])
@@ -126,7 +134,7 @@ def tile_dynamicroutingfusion_pa_kernel(
                     nc.scalar.copy(out=dst[:, part], in_=in_k_order)
 
         def spread_bias():
-            b_ps = psum.tile([P, H], BF16, name="b_ps", tag="bank")
+            b_ps = head_bank().tile([P, H], BF16, name="b_ps", tag="bank")
             for q in range(PER_PARTITION):
                 nc.tensor.transpose(b_ps[:, P * q : P * (q + 1)], bias_cols[:, q : q + 1].to_broadcast([P, P]), ident_bf[:])
             nc.scalar.copy(
@@ -135,14 +143,14 @@ def tile_dynamicroutingfusion_pa_kernel(
             )
 
         def spread_vision_of_group_0():
-            v_ps = psum.tile([P, H], BF16, name="v_ps", tag="bank")
+            v_ps = head_bank().tile([P, H], BF16, name="v_ps", tag="bank")
             for hf in range(2):
                 cols = slice(BANK * hf, BANK * (hf + 1))
                 nc.tensor.matmul(out=v_ps[:, cols], lhsT=pick[:], rhs=vision_rows[:, cols], start=True, stop=True)
             nc.scalar.copy(out=vision[:, 0, :], in_=v_ps[:])
 
         def turn(rows_as_words, grouped_as_words):
-            t_ps = psum.tile([P, BANK], F32, name="t_ps", tag="bank")
+            t_ps = head_bank().tile([P, BANK], F32, name="t_ps", tag="bank")
             for i in range(2):
                 for u in range(2):
                     slot = 2 * i + u
@@ -180,22 +188,21 @@ def tile_dynamicroutingfusion_pa_kernel(
         products_of = {}
         softmax_of = {}
 
-        def project_group(g):
-            for c, hf in BANK_ORDER:
-                p_ps = psum.tile([P, BANK], F32, name="p_ps", tag="bank")
-                for i in range(2):
-                    x_cols = slice(TILE_CODES * c + P * i, TILE_CODES * c + P * (i + 1))
-                    w_cols = slice(BANK * i, BANK * (i + 1))
-                    nc.tensor.matmul_mx(
-                        out=p_ps[:],
-                        lhsT=x_codes[g][:, x_cols].bitcast(FP8X4),
-                        lhsT_scale=x_scales[g][:, x_cols],
-                        rhs=w_codes[hf][:, w_cols].bitcast(FP8X4),
-                        rhs_scale=w_scales[hf][:, w_cols],
-                        start=(i == 0),
-                        stop=(i == 1),
-                    )
-                bank_of[(g, c, hf)] = p_ps
+        def project(g, c, hf):
+            p_ps = (uppers if hf else lowers).tile([P, BANK], F32, name="p_ps", tag="bank")
+            for i in range(2):
+                x_cols = slice(TILE_CODES * c + P * i, TILE_CODES * c + P * (i + 1))
+                w_cols = slice(BANK * i, BANK * (i + 1))
+                nc.tensor.matmul_mx(
+                    out=p_ps[:],
+                    lhsT=x_codes[g][:, x_cols].bitcast(FP8X4),
+                    lhsT_scale=x_scales[g][:, x_cols],
+                    rhs=w_codes[hf][:, w_cols].bitcast(FP8X4),
+                    rhs_scale=w_scales[hf][:, w_cols],
+                    start=(i == 0),
+                    stop=(i == 1),
+                )
+            bank_of[(g, c, hf)] = p_ps
 
         def open_group(g):
             for c in range(2):
@@ -256,15 +263,18 @@ def tile_dynamicroutingfusion_pa_kernel(
                 op0=ALU.mult, op1=ALU.mult, accum_out=partial[:, 2 * c + hf : 2 * c + hf + 1],
             )
 
-        def gather_batch(g):
+        def place_values(g):
             minus_2a = softmax_of[(g, "minus_2a")]
             placed = small.tile([P, 2 * SPAN], F32, name="placed")
             for c in range(2):
                 nc.scalar.activation(
                     out=placed[:, SPAN * c : SPAN * (c + 1)], in_=place[:], func=ACT.Copy, scale=minus_2a[:, c : c + 1]
                 )
-            own = psum.tile([P, 2 * SPAN], F32, name="own", tag="bank")
-            nc.tensor.matmul(out=own[:], lhsT=same_batch[:], rhs=placed[:], start=True, stop=True)
+            softmax_of[(g, "placed")] = placed
+
+        def gather_batch(g):
+            own = owns.tile([P, 2 * SPAN], F32, name="own")
+            nc.tensor.matmul(out=own[:], lhsT=same_batch[:], rhs=softmax_of[(g, "placed")][:], start=True, stop=True)
             softmax_of[(g, "own")] = own
 
         def exponentials(g):
@@ -357,10 +367,12 @@ def tile_dynamicroutingfusion_pa_kernel(
             spread_vision_of_group_0()
             quantize_w(1)
             quantize_w(0)
-            project_group(0)
+            for c, hf in BANK_ORDER:
+                project(0, c, hf)
             quantize_x(2)
             quantize_x(3)
-            project_group(1)
+            for c, hf in BANK_ORDER[0:3]:
+                project(1, c, hf)
 
             open_group(0)
             open_products(0)
@@ -369,6 +381,9 @@ def tile_dynamicroutingfusion_pa_kernel(
             for g in range(LAST):
                 add_bias_and_store(g, 1, 1)
                 multiply_on_gpsimd(g, 1)
+                if g + 2 < GROUPS:
+                    project(g + 2, 0, 1)
+                    project(g + 2, 1, 1)
                 multiply_on_vector(g, 0)
                 sum_on_scalar(g, 0)
                 multiply_on_vector(g, 1)
@@ -379,9 +394,13 @@ def tile_dynamicroutingfusion_pa_kernel(
                 open_products(g + 1)
                 add_bias_and_store(g + 1, 0, 1)
                 multiply_on_gpsimd(g + 1, 0)
-                gather_batch(g)
+                place_values(g)
                 add_bias_and_store(g, 0, 0)
+                project(g + 1, 1, 0)
                 add_bias_and_store(g, 1, 0)
+                if g + 2 < GROUPS:
+                    project(g + 2, 0, 0)
+                gather_batch(g)
                 if g + 1 == LAST:
                     add_bias_and_store(LAST, 1, 1)
                     multiply_on_gpsimd(LAST, 1)
@@ -390,27 +409,27 @@ def tile_dynamicroutingfusion_pa_kernel(
                     weighted_1 = weigh_group(g - 1, g < LAST - 1)
                     if g < LAST - 1:
                         store_weighted(weighted_1, g - 1, 1, slice(0, H))
-                if g + 2 < GROUPS:
-                    project_group(g + 2)
 
             partial = keep.tile([P, 4], F32, name="partial")
             multiply_and_sum_on_vector(partial, LAST, 0, 0)
             multiply_and_sum_on_vector(partial, LAST, 1, 0)
             sum_upper_on_scalar(partial, LAST, 0)
-            exponentials(LAST - 1)
             sum_upper_on_scalar(partial, LAST, 1)
-            add_bias_and_store(LAST, 0, 0)
-            routing_on_scalar(LAST - 1)
-            store_weighted(weighted_1, LAST - 2, 1, slice(0, H))
             weigh_on_vector(LAST - 2, 0)
+            exponentials(LAST - 1)
             nc.vector.tensor_tensor(
                 out=softmax_of[(LAST, "minus_2a")][:], in0=partial[:, 0:4:2], in1=partial[:, 1:4:2], op=ALU.add
             )
+            place_values(LAST)
             gather_batch(LAST)
-            weighted_1 = weigh_group(LAST - 1)
+            add_bias_and_store(LAST, 0, 0)
+            store_weighted(weighted_1, LAST - 2, 1, slice(0, H))
+            routing_on_scalar(LAST - 1)
+            weighted_1 = weigh_group(LAST - 1, False)
             add_bias_and_store(LAST, 1, 0)
-            store_weighted(weighted_1, LAST - 1, 1, slice(0, H))
             exponentials(LAST)
+            weigh_on_vector(LAST - 1, 0)
+            store_weighted(weighted_1, LAST - 1, 1, slice(0, H))
             routing_on_vector(LAST)
             weigh_on_vector(LAST, 1)
             weighted_0 = outs.tile([P, H], F32, name="weighted")

@@ -116,14 +116,14 @@ def tile_dynamicroutingfusion_pa_kernel(
 
         banks_taken = [0]
 
-        def head_bank():
+        def pool_of_next_bank():
             banks_taken[0] += 1
             return (uppers, lowers)[banks_taken[0] % 2]
 
         def spread_scales():
             dst = scale_all[:].rearrange("p (r part q) -> p part r q", part=2, q=4)
             for part in range(2):
-                s_ps = head_bank().tile([P, BANK], F32, name="s_ps", tag="bank")
+                s_ps = pool_of_next_bank().tile([P, BANK], F32, name="s_ps", tag="bank")
                 for q in range(4):
                     col = scale_cols[:, 4 * part + q : 4 * part + q + 1]
                     nc.tensor.transpose(s_ps[:, P * q : P * (q + 1)], col.to_broadcast([P, P]), ident[:])
@@ -134,7 +134,7 @@ def tile_dynamicroutingfusion_pa_kernel(
                     nc.scalar.copy(out=dst[:, part], in_=in_k_order)
 
         def spread_bias():
-            b_ps = head_bank().tile([P, H], BF16, name="b_ps", tag="bank")
+            b_ps = pool_of_next_bank().tile([P, H], BF16, name="b_ps", tag="bank")
             for q in range(PER_PARTITION):
                 nc.tensor.transpose(b_ps[:, P * q : P * (q + 1)], bias_cols[:, q : q + 1].to_broadcast([P, P]), ident_bf[:])
             nc.scalar.copy(
@@ -143,14 +143,14 @@ def tile_dynamicroutingfusion_pa_kernel(
             )
 
         def spread_vision_of_group_0():
-            v_ps = head_bank().tile([P, H], BF16, name="v_ps", tag="bank")
+            v_ps = pool_of_next_bank().tile([P, H], BF16, name="v_ps", tag="bank")
             for hf in range(2):
                 cols = slice(BANK * hf, BANK * (hf + 1))
                 nc.tensor.matmul(out=v_ps[:, cols], lhsT=pick[:], rhs=vision_rows[:, cols], start=True, stop=True)
             nc.scalar.copy(out=vision[:, 0, :], in_=v_ps[:])
 
         def turn(rows_as_words, grouped_as_words):
-            t_ps = head_bank().tile([P, BANK], F32, name="t_ps", tag="bank")
+            t_ps = pool_of_next_bank().tile([P, BANK], F32, name="t_ps", tag="bank")
             for i in range(2):
                 for u in range(2):
                     slot = 2 * i + u
@@ -216,18 +216,11 @@ def tile_dynamicroutingfusion_pa_kernel(
                 products = prods.tile([P, H], F32, name="products")
                 products_of[(g, c)] = products
 
-        def add_bias(g, c, hf):
+        def add_bias_and_store(g, c, hf):
             cols = slice(BANK * hf, BANK * (hf + 1))
             nc.vector.tensor_tensor(
                 out=text_proj_of[(g, c)][:, cols], in0=bank_of[(g, c, hf)][:], in1=bias_all[:, cols], op=ALU.add
             )
-
-        def store_text_proj(g, c):
-            nc.sync.dma_start(out=text_proj_view[g, c], in_=text_proj_of[(g, c)][:])
-
-        def add_bias_and_store(g, c, hf):
-            add_bias(g, c, hf)
-            cols = slice(BANK * hf, BANK * (hf + 1))
             nc.sync.dma_start(out=text_proj_view[g, c][:, cols], in_=text_proj_of[(g, c)][:, cols])
 
         def multiply_on_vector(g, c):
@@ -312,37 +305,33 @@ def tile_dynamicroutingfusion_pa_kernel(
                 op0=ALU.mult,
             )
 
-        def weigh_on_scalar(weighted, g, c, cols):
+        weighted_of = {}
+
+        def open_weighted(g, c):
+            weighted = outs.tile([P, H], F32, name="weighted")
+            weighted_of[(g, c)] = weighted
+
+        def weigh_and_store_on_scalar(g, c, cols):
             nc.scalar.activation(
-                out=weighted[:, cols], in_=vision[:, g, cols], func=ACT.Copy,
+                out=weighted_of[(g, c)][:, cols], in_=vision[:, g, cols], func=ACT.Copy,
                 scale=softmax_of[(g, "routing")][:, c : c + 1],
             )
-            nc.scalar.dma_start(out=weighted_view[g, c][:, cols], in_=weighted[:, cols])
+            nc.scalar.dma_start(out=weighted_view[g, c][:, cols], in_=weighted_of[(g, c)][:, cols])
 
-        def weigh_on_gpsimd(weighted, g, c, cols):
+        def weigh_on_gpsimd(g, c, cols):
             nc.gpsimd.tensor_scalar(
-                out=weighted[:, cols], in0=vision[:, g, cols], scalar1=softmax_of[(g, "routing")][:, c : c + 1],
+                out=weighted_of[(g, c)][:, cols], in0=vision[:, g, cols], scalar1=softmax_of[(g, "routing")][:, c : c + 1],
                 scalar2=0.0, op0=ALU.mult, op1=ALU.add,
             )
 
         def weigh_on_vector(g, c):
-            weighted = outs.tile([P, H], F32, name="weighted")
             nc.vector.tensor_scalar(
-                out=weighted[:], in0=vision[:, g, :], scalar1=softmax_of[(g, "routing")][:, c : c + 1], scalar2=None,
-                op0=ALU.mult,
+                out=weighted_of[(g, c)][:], in0=vision[:, g, :], scalar1=softmax_of[(g, "routing")][:, c : c + 1],
+                scalar2=None, op0=ALU.mult,
             )
-            store_weighted(weighted, g, c, slice(0, H))
 
-        def weigh_group(g, both=True):
-            if both:
-                weighted_0 = outs.tile([P, H], F32, name="weighted")
-                weigh_on_scalar(weighted_0, g, 0, slice(0, H))
-            weighted_1 = outs.tile([P, H], F32, name="weighted")
-            weigh_on_gpsimd(weighted_1, g, 1, slice(0, H))
-            return weighted_1
-
-        def store_weighted(weighted, g, c, cols):
-            nc.sync.dma_start(out=weighted_view[g, c][:, cols], in_=weighted[:, cols])
+        def store_weighted(g, c, cols):
+            nc.sync.dma_start(out=weighted_view[g, c][:, cols], in_=weighted_of[(g, c)][:, cols])
 
         with tc.manual_schedule():
             spread_scales()
@@ -374,6 +363,7 @@ def tile_dynamicroutingfusion_pa_kernel(
             for c, hf in BANK_ORDER[0:3]:
                 project(1, c, hf)
 
+            whole = slice(0, H)
             open_group(0)
             open_products(0)
             add_bias_and_store(0, 0, 1)
@@ -386,6 +376,8 @@ def tile_dynamicroutingfusion_pa_kernel(
                     project(g + 2, 1, 1)
                 multiply_on_vector(g, 0)
                 sum_on_scalar(g, 0)
+                add_bias_and_store(g, 0, 0)
+                project(g + 1, 1, 0)
                 multiply_on_vector(g, 1)
                 if g > 0:
                     exponentials(g - 1)
@@ -395,44 +387,53 @@ def tile_dynamicroutingfusion_pa_kernel(
                 add_bias_and_store(g + 1, 0, 1)
                 multiply_on_gpsimd(g + 1, 0)
                 place_values(g)
-                add_bias_and_store(g, 0, 0)
-                project(g + 1, 1, 0)
                 add_bias_and_store(g, 1, 0)
                 if g + 2 < GROUPS:
                     project(g + 2, 0, 0)
                 gather_batch(g)
-                if g + 1 == LAST:
-                    add_bias_and_store(LAST, 1, 1)
-                    multiply_on_gpsimd(LAST, 1)
-                if g > 0:
-                    routing_on_scalar(g - 1)
-                    weighted_1 = weigh_group(g - 1, g < LAST - 1)
-                    if g < LAST - 1:
-                        store_weighted(weighted_1, g - 1, 1, slice(0, H))
+                if g == 1:
+                    routing_on_scalar(0)
+                    open_weighted(0, 0)
+                    weigh_and_store_on_scalar(0, 0, whole)
+                    open_weighted(0, 1)
+                    weigh_on_gpsimd(0, 1, whole)
+                    store_weighted(0, 1, whole)
+            add_bias_and_store(LAST, 1, 1)
+            multiply_on_gpsimd(LAST, 1)
+            routing_on_scalar(1)
+            open_weighted(1, 1)
+            weigh_on_gpsimd(1, 1, whole)
 
             partial = keep.tile([P, 4], F32, name="partial")
             multiply_and_sum_on_vector(partial, LAST, 0, 0)
             multiply_and_sum_on_vector(partial, LAST, 1, 0)
             sum_upper_on_scalar(partial, LAST, 0)
             sum_upper_on_scalar(partial, LAST, 1)
-            weigh_on_vector(LAST - 2, 0)
-            exponentials(LAST - 1)
+            open_weighted(1, 0)
+            weigh_on_vector(1, 0)
+            store_weighted(1, 0, whole)
+            exponentials(2)
             nc.vector.tensor_tensor(
                 out=softmax_of[(LAST, "minus_2a")][:], in0=partial[:, 0:4:2], in1=partial[:, 1:4:2], op=ALU.add
             )
             place_values(LAST)
             gather_batch(LAST)
             add_bias_and_store(LAST, 0, 0)
-            store_weighted(weighted_1, LAST - 2, 1, slice(0, H))
-            routing_on_scalar(LAST - 1)
-            weighted_1 = weigh_group(LAST - 1, False)
+            store_weighted(1, 1, whole)
+            routing_on_scalar(2)
+            open_weighted(2, 1)
+            weigh_on_gpsimd(2, 1, whole)
             add_bias_and_store(LAST, 1, 0)
             exponentials(LAST)
-            weigh_on_vector(LAST - 1, 0)
-            store_weighted(weighted_1, LAST - 1, 1, slice(0, H))
+            open_weighted(2, 0)
+            weigh_on_vector(2, 0)
+            store_weighted(2, 0, whole)
+            store_weighted(2, 1, whole)
             routing_on_vector(LAST)
+            open_weighted(LAST, 1)
             weigh_on_vector(LAST, 1)
-            weighted_0 = outs.tile([P, H], F32, name="weighted")
-            weigh_on_scalar(weighted_0, LAST, 0, slice(0, BANK))
-            weigh_on_gpsimd(weighted_0, LAST, 0, slice(BANK, H))
-            store_weighted(weighted_0, LAST, 0, slice(BANK, H))
+            store_weighted(LAST, 1, whole)
+            open_weighted(LAST, 0)
+            weigh_and_store_on_scalar(LAST, 0, slice(0, BANK))
+            weigh_on_gpsimd(LAST, 0, slice(BANK, H))
+            store_weighted(LAST, 0, slice(BANK, H))

from contextlib import ExitStack

import concourse.mybir as mybir
from concourse.masks import make_block_diagonal, make_identity

FLOPS = 2 * 1024 * 1024 * 1024

F32 = mybir.dt.float32
BF16 = mybir.dt.bfloat16
U32 = mybir.dt.uint32
U8 = mybir.dt.uint8
FP8 = mybir.dt.float8_e4m3fn
FP8X4 = mybir.dt.float8_e4m3fn_x4
ALU = mybir.AluOpType
ACT = mybir.ActivationFunctionType
AX = mybir.AxisListType

P = 128
H = 1024
BANK = 512
GROUPS = 4
LAST = GROUPS - 1
SPAN = 16
BATCHES = P // SPAN
W_TILES = H // P
PER_PARTITION = H // P
PASS_WORDS = 256
TILE_CODES = 2 * P
BANK_ORDER = ((0, 1), (1, 1), (0, 0), (1, 0))
W_TILES_BEFORE = (3, 1, 2, 2)


def tile_dynamicroutingfusion_pa_kernel(
    tc, text_feat_bytes, text_feat_scale, vision_proj, Wt, bt, out_0, out_1
):
    nc = tc.nc
    with ExitStack() as ctx:
        keep = ctx.enter_context(tc.tile_pool(name="keep", bufs=1))
        outs = ctx.enter_context(tc.tile_pool(name="outs", bufs=6))
        prods = ctx.enter_context(tc.tile_pool(name="prods", bufs=4))
        small = ctx.enter_context(tc.tile_pool(name="small", bufs=2))
        uppers = ctx.enter_context(tc.psum_pool(name="uppers", bufs=4))
        lowers = ctx.enter_context(tc.psum_pool(name="lowers", bufs=3))
        owns = ctx.enter_context(tc.psum_pool(name="owns", bufs=1))

        bytes_view = text_feat_bytes.flatten_outer_dims().rearrange("(g p c) k -> g p (c k)", p=P, c=2)
        text_proj_view = out_0.flatten_outer_dims().rearrange("(g p c) h -> g c p h", p=P, c=2)
        weighted_view = out_1.flatten_outer_dims().rearrange("(g p c) h -> g c p h", p=P, c=2)

        scale_all = keep.tile([P, H], F32, name="scale_all")
        bias_all = keep.tile([P, H], BF16, name="bias_all")
        vision = keep.tile([P, GROUPS, H], BF16, name="vision")
        x_bytes, x_scaled, x_grouped, x_codes, x_scales = [], [], [], [], []
        for g in range(GROUPS):
            x_bytes_g = keep.tile([P, 2 * H], U8, name="x_bytes%d" % g)
            x_scaled_g = keep.tile([P, 2 * H], BF16, name="x_scaled%d" % g)
            x_grouped_g = keep.tile([P, 2 * H], BF16, name="x_grouped%d" % g, align_bytes=64)
            x_codes_g = keep.tile([P, 2 * TILE_CODES], U32, name="x_codes%d" % g, align_bytes=64)
            x_scales_g = keep.tile([P, 2 * TILE_CODES], U8, name="x_scales%d" % g, align_bytes=64)
            x_bytes.append(x_bytes_g)
            x_scaled.append(x_scaled_g)
            x_grouped.append(x_grouped_g)
            x_codes.append(x_codes_g)
            x_scales.append(x_scales_g)
        w_rows = []
        for j in range(W_TILES):
            w_rows_j = keep.tile([P, H], BF16, name="w_rows%d" % j)
            w_rows.append(w_rows_j)
        w_grouped, w_codes, w_scales = [], [], []
        for hf in range(2):
            w_grouped_h = keep.tile([P, 4 * H], BF16, name="w_grouped%d" % hf, align_bytes=64)
            w_codes_h = keep.tile([P, H], U32, name="w_codes%d" % hf, align_bytes=64)
            w_scales_h = keep.tile([P, H], U8, name="w_scales%d" % hf, align_bytes=64)
            w_grouped.append(w_grouped_h)
            w_codes.append(w_codes_h)
            w_scales.append(w_scales_h)

        scale_cols = keep.tile([P, PER_PARTITION], F32, name="scale_cols")
        nc.sync.dma_start(out=scale_cols[:], in_=text_feat_scale.rearrange("a b (p q) -> (a b p) q", q=PER_PARTITION))
        bias_cols = keep.tile([P, PER_PARTITION], BF16, name="bias_cols")
        nc.sync.dma_start(out=bias_cols[:], in_=bt.rearrange("(p q) -> p q", q=PER_PARTITION))
        nc.sync.dma_start(out=x_bytes[0][:], in_=bytes_view[0])
        for j in range(W_TILES):
            nc.sync.dma_start(out=w_rows[j][:], in_=Wt[P * j : P * (j + 1), :])
            if j == W_TILES_BEFORE[0] - 1:
                nc.sync.dma_start(out=x_bytes[1][:], in_=bytes_view[1])
        vision_rows = keep.tile([P, H], BF16, name="vision_rows")
        nc.vector.memset(vision_rows[:], 0.0)
        nc.sync.dma_start(out=vision_rows[0:BATCHES, :], in_=vision_proj[0:BATCHES].rearrange("b o h -> (b o) h"))
        nc.sync.dma_start(out=x_bytes[2][:], in_=bytes_view[2])
        nc.sync.dma_start(out=x_bytes[3][:], in_=bytes_view[3])
        vision_by_batch = vision_proj.rearrange("(g e) o h -> e (o g) h", e=BATCHES)
        for low in range(4):
            for high in range(4):
                r = 4 * high + low
                nc.sync.dma_start(out=vision[r:P:SPAN, 1:GROUPS, :], in_=vision_by_batch[:, 1:GROUPS, :])

        ident = keep.tile([P, P], F32, name="ident")
        make_identity(nc, ident[:])
        zero = keep.tile([P, 1], F32, name="zero")
        nc.vector.memset(zero[:], 0.0)
        warm = keep.tile([P, 1], F32, name="warm")
        nc.scalar.activation(out=warm[:], in_=zero[:], func=ACT.Exp)
        ident_bf = keep.tile([P, P], BF16, name="ident_bf")
        make_identity(nc, ident_bf[:])
        pick = keep.tile([P, P], BF16, name="pick")
        nc.gpsimd.memset(pick[:], 0.0)
        nc.gpsimd.affine_select(
            out=pick[:], in_=pick[:], compare_op=ALU.not_equal, fill=1.0, base=0,
            pattern=[[-1, BATCHES], [0, SPAN]], channel_multiplier=1,
        )
        same_batch = keep.tile([P, P], F32, name="same_batch")
        make_block_diagonal(nc, same_batch[:], SPAN)
        place = keep.tile([P, SPAN], F32, name="place")
        nc.vector.tensor_reduce(out=place[:], in_=ident[:].rearrange("p (e n) -> p n e", n=SPAN), axis=AX.X, op=ALU.add)

        banks_taken = [0]

        def pool_of_next_bank():
            banks_taken[0] += 1
            return (uppers, lowers)[banks_taken[0] % 2]

        def spread_scales():
            dst = scale_all[:].rearrange("p (r part q) -> p part r q", part=2, q=4)
            for part in range(2):
                s_ps = pool_of_next_bank().tile([P, BANK], F32, name="s_ps", tag="bank")
                for q in range(4):
                    col = scale_cols[:, 4 * part + q : 4 * part + q + 1]
                    nc.tensor.transpose(s_ps[:, P * q : P * (q + 1)], col.to_broadcast([P, P]), ident[:])
                in_k_order = s_ps[:].rearrange("p (q r) -> p r q", q=4)
                if part == 0:
                    nc.vector.tensor_copy(out=dst[:, part], in_=in_k_order)
                else:
                    nc.scalar.copy(out=dst[:, part], in_=in_k_order)

        def spread_bias():
            b_ps = pool_of_next_bank().tile([P, H], BF16, name="b_ps", tag="bank")
            for q in range(PER_PARTITION):
                nc.tensor.transpose(b_ps[:, P * q : P * (q + 1)], bias_cols[:, q : q + 1].to_broadcast([P, P]), ident_bf[:])
            nc.scalar.copy(
                out=bias_all[:].rearrange("p (r q) -> p r q", q=PER_PARTITION),
                in_=b_ps[:].rearrange("p (q r) -> p r q", q=PER_PARTITION),
            )

        def spread_vision_of_group_0():
            v_ps = pool_of_next_bank().tile([P, H], BF16, name="v_ps", tag="bank")
            for hf in range(2):
                cols = slice(BANK * hf, BANK * (hf + 1))
                nc.tensor.matmul(out=v_ps[:, cols], lhsT=pick[:], rhs=vision_rows[:, cols], start=True, stop=True)
            nc.scalar.copy(out=vision[:, 0, :], in_=v_ps[:])

        def turn(rows_as_words, grouped_as_words):
            t_ps = pool_of_next_bank().tile([P, BANK], F32, name="t_ps", tag="bank")
            for i in range(2):
                for u in range(2):
                    slot = 2 * i + u
                    nc.tensor.transpose(
                        t_ps[:, P * slot : P * (slot + 1)],
                        rows_as_words[:, PASS_WORDS * i + u : PASS_WORDS * (i + 1) : 2],
                        ident[:],
                    )
            nc.scalar.copy(out=grouped_as_words, in_=t_ps[:].rearrange("p (i u r) -> p i r u", i=2, u=2))

        def turn_w(j):
            hf, place_in_half = divmod(j, W_TILES // 2)
            dst = w_grouped[hf][:].bitcast(F32).rearrange("p (i h u) -> p i h u", i=2, u=2)
            turn(w_rows[j][:].bitcast(F32), dst[:, :, P * place_in_half : P * (place_in_half + 1), :])

        def quantize_w(hf):
            nc.vector.quantize_mx(out=w_codes[hf][:].bitcast(FP8X4), scales=w_scales[hf][:], in_=w_grouped[hf][:])

        def widen_x(g, c):
            cols = slice(H * c, H * (c + 1))
            nc.vector.tensor_tensor(
                out=x_scaled[g][:, cols], in0=x_bytes[g][:, cols].bitcast(FP8), in1=scale_all[:], op=ALU.mult
            )

        def turn_x(g, c):
            cols = slice(H * c, H * (c + 1))
            dst = x_grouped[g][:, cols].bitcast(F32).rearrange("p (i r u) -> p i r u", i=2, u=2)
            turn(x_scaled[g][:, cols].bitcast(F32), dst)

        def quantize_x(g):
            nc.vector.quantize_mx(out=x_codes[g][:].bitcast(FP8X4), scales=x_scales[g][:], in_=x_grouped[g][:])

        bank_of = {}
        text_proj_of = {}
        products_of = {}
        softmax_of = {}

        def project(g, c, hf):
            p_ps = (uppers if hf else lowers).tile([P, BANK], F32, name="p_ps", tag="bank")
            for i in range(2):
                x_cols = slice(TILE_CODES * c + P * i, TILE_CODES * c + P * (i + 1))
                w_cols = slice(BANK * i, BANK * (i + 1))
                nc.tensor.matmul_mx(
                    out=p_ps[:],
                    lhsT=x_codes[g][:, x_cols].bitcast(FP8X4),
                    lhsT_scale=x_scales[g][:, x_cols],
                    rhs=w_codes[hf][:, w_cols].bitcast(FP8X4),
                    rhs_scale=w_scales[hf][:, w_cols],
                    start=(i == 0),
                    stop=(i == 1),
                )
            bank_of[(g, c, hf)] = p_ps

        def open_group(g):
            for c in range(2):
                text_proj = outs.tile([P, H], F32, name="text_proj")
                text_proj_of[(g, c)] = text_proj
            minus_2a = small.tile([P, 2], F32, name="minus_2a")
            softmax_of[(g, "minus_2a")] = minus_2a

        def open_products(g):
            for c in range(2):
                products = prods.tile([P, H], F32, name="products")
                products_of[(g, c)] = products

        def add_bias_and_store(g, c, hf):
            cols = slice(BANK * hf, BANK * (hf + 1))
            nc.vector.tensor_tensor(
                out=text_proj_of[(g, c)][:, cols], in0=bank_of[(g, c, hf)][:], in1=bias_all[:, cols], op=ALU.add
            )
            nc.sync.dma_start(out=text_proj_view[g, c][:, cols], in_=text_proj_of[(g, c)][:, cols])

        def multiply_on_vector(g, c):
            nc.vector.tensor_tensor(
                out=products_of[(g, c)][:, 0:BANK], in0=bank_of[(g, c, 0)][:], in1=vision[:, g, 0:BANK], op=ALU.mult
            )

        def multiply_on_gpsimd(g, c):
            nc.gpsimd.tensor_tensor(
                out=products_of[(g, c)][:, BANK:H], in0=text_proj_of[(g, c)][:, BANK:H], in1=vision[:, g, BANK:H],
                op=ALU.mult,
            )

        def sum_on_scalar(g, c):
            unused = small.tile([P, H], BF16, name="unused")
            nc.scalar.activation(
                out=unused[:], in_=products_of[(g, c)][:], func=ACT.Copy, scale=-2.0,
                accum_out=softmax_of[(g, "minus_2a")][:, c : c + 1],
            )

        def sum_upper_on_scalar(partial, g, c):
            unused = small.tile([P, H], BF16, name="unused")
            nc.scalar.activation(
                out=unused[:, BANK:H], in_=products_of[(g, c)][:, BANK:H], func=ACT.Copy, scale=-2.0,
                accum_out=partial[:, 2 * c + 1 : 2 * c + 2],
            )

        def multiply_and_sum_on_vector(partial, g, c, hf):
            cols = slice(BANK * hf, BANK * (hf + 1))
            unused_half = small.tile([P, BANK], BF16, name="unused_half")
            nc.vector.scalar_tensor_tensor(
                out=unused_half[:], in0=bank_of[(g, c, hf)][:], scalar=-2.0, in1=vision[:, g, cols],
                op0=ALU.mult, op1=ALU.mult, accum_out=partial[:, 2 * c + hf : 2 * c + hf + 1],
            )

        def place_values(g):
            minus_2a = softmax_of[(g, "minus_2a")]
            placed = small.tile([P, 2 * SPAN], F32, name="placed")
            for c in range(2):
                nc.scalar.activation(
                    out=placed[:, SPAN * c : SPAN * (c + 1)], in_=place[:], func=ACT.Copy, scale=minus_2a[:, c : c + 1]
                )
            softmax_of[(g, "placed")] = placed

        def gather_batch(g):
            own = owns.tile([P, 2 * SPAN], F32, name="own")
            nc.tensor.matmul(out=own[:], lhsT=same_batch[:], rhs=softmax_of[(g, "placed")][:], start=True, stop=True)
            softmax_of[(g, "own")] = own

        def exponentials(g):
            minus_m = small.tile([P, 1], F32, name="minus_m")
            nc.vector.tensor_reduce(out=minus_m[:], in_=softmax_of[(g, "own")][:], axis=AX.X, op=ALU.min)
            terms = small.tile([P, 2 * SPAN], F32, name="terms")
            den = small.tile([P, 1], F32, name="den")
            nc.scalar.activation(
                out=terms[:], in_=softmax_of[(g, "own")][:], func=ACT.Exp, bias=minus_m[:], scale=-1.0, accum_out=den[:]
            )
            num = small.tile([P, 2], F32, name="num")
            nc.scalar.activation(
                out=num[:], in_=softmax_of[(g, "minus_2a")][:], func=ACT.Exp, bias=minus_m[:], scale=-1.0
            )
            softmax_of[(g, "den")] = den
            softmax_of[(g, "num")] = num

        def reciprocal_of_den(g):
            inv_den = small.tile([P, 1], F32, name="inv_den")
            nc.vector.reciprocal(out=inv_den[:], in_=softmax_of[(g, "den")][:])
            routing = small.tile([P, 2], F32, name="routing")
            softmax_of[(g, "routing")] = routing
            return inv_den

        def routing_on_scalar(g):
            inv_den = reciprocal_of_den(g)
            nc.scalar.activation(
                out=softmax_of[(g, "routing")][:], in_=softmax_of[(g, "num")][:], func=ACT.Copy, scale=inv_den[:, 0:1]
            )

        def routing_on_vector(g):
            inv_den = reciprocal_of_den(g)
            nc.vector.tensor_scalar(
                out=softmax_of[(g, "routing")][:], in0=softmax_of[(g, "num")][:], scalar1=inv_den[:, 0:1], scalar2=None,
                op0=ALU.mult,
            )

        weighted_of = {}

        def open_weighted(g, c):
            weighted = outs.tile([P, H], F32, name="weighted")
            weighted_of[(g, c)] = weighted

        def weigh_and_store_on_scalar(g, c, cols):
            nc.scalar.activation(
                out=weighted_of[(g, c)][:, cols], in_=vision[:, g, cols], func=ACT.Copy,
                scale=softmax_of[(g, "routing")][:, c : c + 1],
            )
            nc.scalar.dma_start(out=weighted_view[g, c][:, cols], in_=weighted_of[(g, c)][:, cols])

        def weigh_on_gpsimd(g, c, cols):
            nc.gpsimd.tensor_scalar(
                out=weighted_of[(g, c)][:, cols], in0=vision[:, g, cols], scalar1=softmax_of[(g, "routing")][:, c : c + 1],
                scalar2=0.0, op0=ALU.mult, op1=ALU.add,
            )

        def weigh_on_vector(g, c):
            nc.vector.tensor_scalar(
                out=weighted_of[(g, c)][:], in0=vision[:, g, :], scalar1=softmax_of[(g, "routing")][:, c : c + 1],
                scalar2=None, op0=ALU.mult,
            )

        def store_weighted(g, c, cols):
            nc.sync.dma_start(out=weighted_view[g, c][:, cols], in_=weighted_of[(g, c)][:, cols])

        with tc.manual_schedule():
            spread_scales()
            j = 0
            for tile_no in range(len(W_TILES_BEFORE)):
                for count in range(W_TILES_BEFORE[tile_no]):
                    turn_w(j)
                    j += 1
                widen_x(tile_no // 2, tile_no % 2)
                turn_x(tile_no // 2, tile_no % 2)
            quantize_x(0)
            widen_x(2, 0)
            turn_x(2, 0)
            widen_x(2, 1)
            turn_x(2, 1)
            spread_bias()
            widen_x(3, 0)
            quantize_x(1)
            turn_x(3, 0)
            widen_x(3, 1)
            turn_x(3, 1)
            spread_vision_of_group_0()
            quantize_w(1)
            quantize_w(0)
            for c, hf in BANK_ORDER:
                project(0, c, hf)
            quantize_x(2)
            quantize_x(3)
            for c, hf in BANK_ORDER[0:3]:
                project(1, c, hf)

            whole = slice(0, H)
            open_group(0)
            open_products(0)
            add_bias_and_store(0, 0, 1)
            multiply_on_gpsimd(0, 0)
            for g in range(LAST):
                add_bias_and_store(g, 1, 1)
                multiply_on_gpsimd(g, 1)
                if g + 2 < GROUPS:
                    project(g + 2, 0, 1)
                    project(g + 2, 1, 1)
                multiply_on_vector(g, 0)
                sum_on_scalar(g, 0)
                add_bias_and_store(g, 0, 0)
                project(g + 1, 1, 0)
                multiply_on_vector(g, 1)
                if g > 0:
                    exponentials(g - 1)
                sum_on_scalar(g, 1)
                open_group(g + 1)
                open_products(g + 1)
                add_bias_and_store(g + 1, 0, 1)
                multiply_on_gpsimd(g + 1, 0)
                place_values(g)
                add_bias_and_store(g, 1, 0)
                if g + 2 < GROUPS:
                    project(g + 2, 0, 0)
                gather_batch(g)
                if g == 1:
                    routing_on_scalar(0)
                    open_weighted(0, 0)
                    weigh_and_store_on_scalar(0, 0, whole)
                    open_weighted(0, 1)
                    weigh_on_gpsimd(0, 1, whole)
                    store_weighted(0, 1, whole)
            add_bias_and_store(LAST, 1, 1)
            multiply_on_gpsimd(LAST, 1)
            routing_on_scalar(1)
            open_weighted(1, 1)
            weigh_on_gpsimd(1, 1, whole)

            partial = keep.tile([P, 4], F32, name="partial")
            multiply_and_sum_on_vector(partial, LAST, 0, 0)
            multiply_and_sum_on_vector(partial, LAST, 1, 0)
            sum_upper_on_scalar(partial, LAST, 0)
            sum_upper_on_scalar(partial, LAST, 1)
            open_weighted(1, 0)
            weigh_on_vector(1, 0)
            store_weighted(1, 0, whole)
            exponentials(2)
            nc.vector.tensor_tensor(
                out=softmax_of[(LAST, "minus_2a")][:], in0=partial[:, 0:4:2], in1=partial[:, 1:4:2], op=ALU.add
            )
            place_values(LAST)
            gather_batch(LAST)
            add_bias_and_store(LAST, 0, 0)
            store_weighted(1, 1, whole)
            routing_on_scalar(2)
            open_weighted(2, 1)
            weigh_on_gpsimd(2, 1, whole)
            add_bias_and_store(LAST, 1, 0)
            exponentials(LAST)
            open_weighted(2, 0)
            weigh_on_vector(2, 0)
            store_weighted(2, 0, whole)
            store_weighted(2, 1, whole)
            routing_on_vector(LAST)
            open_weighted(LAST, 1)
            weigh_on_vector(LAST, 1)
            store_weighted(LAST, 1, whole)
            open_weighted(LAST, 0)
            weigh_and_store_on_scalar(LAST, 0, slice(0, BANK))
            weigh_on_gpsimd(LAST, 0, slice(BANK, H))
            store_weighted(LAST, 0, slice(BANK, H))
